import numpy as np
import ml_dtypes

BF16 = ml_dtypes.bfloat16


def bf(x):
    return np.asarray(x, np.float32).astype(BF16)


def f32(x):
    return np.asarray(x, np.float32)


def f64(x):
    return np.asarray(x).astype(np.float64)


def striped(idx):
    return np.tile(idx.reshape(-1, 16).T, (8, 1))


C, DD, S, N = 384, 128, 4096, 1024
B_CROSS = 0.25


def setup_inputs():
    return {"table": f32(np.random.standard_normal((C, S))), "dense": f32(np.random.standard_normal((DD, N))), "w": f32(np.random.standard_normal((C + DD, 1)) / np.sqrt(C + DD)), "offs": striped(np.random.permutation(np.tile(np.arange(S), 2))[:N])}


def reference(table, dense, w, offs):
    idx = offs[:16].T.reshape(-1)
    x0 = np.concatenate([f64(table)[:, idx], f64(dense)], axis=0)
    s = (f64(w) * x0).sum(axis=0, keepdims=True)
    return x0 * (1.0 + s) + B_CROSS

@@ -1,0 +1,71 @@
+import concourse.mybir as mybir
+
+F32 = mybir.dt.float32
+U16 = mybir.dt.uint16
+MULT = mybir.AluOpType.mult
+COPY = mybir.ActivationFunctionType.Copy
+
+P = 128
+C, DD, S, N = 384, 128, 4096, 1024
+B_CROSS = 0.25
+BLOCKS = C // P
+PIECE = 512
+PIECES = N // PIECE
+LIST_COLS = PIECE // 16
+
+FLOPS = 4 * (C + DD) * N
+
+
+def tile_dcn_kernel(tc, table, dense, w, offs, out):
+    nc = tc.nc
+    with (
+        tc.tile_pool(name="held", bufs=1) as held,
+        tc.tile_pool(name="weighted_pool", bufs=3) as weighted_pool,
+        tc.tile_pool(name="crossed_pool", bufs=4) as crossed_pool,
+        tc.psum_pool(name="outer_psum", bufs=2) as outer_psum,
+        tc.psum_pool(name="sum_psum", bufs=1) as sum_psum,
+    ):
+        offsets = held.tile([P, N // 16], U16, name="offsets")
+        nc.sync.dma_start(offsets[:], offs)
+        windows = [held.tile([P, S], F32, name=f"window{b}") for b in range(BLOCKS)]
+        for b in range(BLOCKS):
+            nc.sync.dma_start(windows[b][:], table[b * P : (b + 1) * P, :])
+        w_row = held.tile([1, C + DD], F32, name="w_row")
+        nc.scalar.dma_start(w_row[:], w.rearrange("c o -> o c"))
+        dense_sb = held.tile([P, N], F32, name="dense_sb")
+        nc.scalar.dma_start(dense_sb[:], dense)
+
+        ones = held.tile([P, PIECE], F32, name="ones")
+        nc.vector.memset(ones[:], 1.0)
+        w_wide = [held.tile([P, PIECE], F32, name=f"w_wide{b}") for b in range(BLOCKS + 1)]
+        for b in range(BLOCKS + 1):
+            w_outer = outer_psum.tile([P, PIECE], F32, name="w_outer")
+            nc.tensor.matmul(w_outer[:], w_row[0:1, b * P : (b + 1) * P], ones[0:1, :], start=True, stop=True)
+            nc.scalar.copy(w_wide[b][:], w_outer[:])
+
+        def piece_of(tile, q):
+            return tile[:, q * PIECE : (q + 1) * PIECE]
+
+        def looked_up(b, q):
+            return windows[b][:].indirect(offsets[:, q * LIST_COLS : (q + 1) * LIST_COLS])
+
+        sums = [sum_psum.tile([P, PIECE], F32, name=f"sum{q}") for q in range(PIECES)]
+        for q in range(PIECES):
+            nc.tensor.matmul(sums[q][:], w_wide[BLOCKS][:, 0:P], piece_of(dense_sb, q), start=True, stop=False)
+        for b in range(BLOCKS):
+            for q in range(PIECES):
+                weighted = weighted_pool.tile([P, PIECE], F32, name="weighted")
+                nc.vector.tensor_tensor(weighted[:], looked_up(b, q), w_wide[b][:], MULT)
+                nc.tensor.matmul(sums[q][:], ones[:, 0:P], weighted[:], start=False, stop=(b == BLOCKS - 1))
+
+        for q in range(PIECES):
+            scale = held.tile([P, PIECE], F32, name=f"scale{q}")
+            nc.scalar.activation(scale[:], sums[q][:], COPY, bias=1.0)
+            for b in range(BLOCKS + 1):
+                crossed = crossed_pool.tile([P, PIECE], F32, name="crossed")
+                if b < BLOCKS:
+                    nc.vector.tensor_tensor(crossed[:], looked_up(b, q), scale[:], MULT)
+                else:
+                    nc.gpsimd.tensor_tensor(crossed[:], piece_of(dense_sb, q), scale[:], MULT)
+                nc.scalar.activation(crossed[:], crossed[:], COPY, bias=B_CROSS)
+                nc.sync.dma_start(piece_of(out[b * P : (b + 1) * P, :], q), crossed[:])

@@ -9,7 +9,7 @@ P = 128
 C, DD, S, N = 384, 128, 4096, 1024
 B_CROSS = 0.25
 BLOCKS = C // P
-PIECE = 512
+PIECE = 256
 PIECES = N // PIECE
 LIST_COLS = PIECE // 16
 
@@ -20,9 +20,9 @@ def tile_dcn_kernel(tc, table, dense, w, offs, out):
     nc = tc.nc
     with (
         tc.tile_pool(name="held", bufs=1) as held,
-        tc.tile_pool(name="weighted_pool", bufs=3) as weighted_pool,
-        tc.tile_pool(name="crossed_pool", bufs=4) as crossed_pool,
-        tc.psum_pool(name="outer_psum", bufs=2) as outer_psum,
+        tc.tile_pool(name="weighted_pool", bufs=PIECES) as weighted_pool,
+        tc.tile_pool(name="crossed_pool", bufs=PIECES * (BLOCKS + 1)) as crossed_pool,
+        tc.psum_pool(name="w_psum_pool", bufs=1) as w_psum_pool,
         tc.psum_pool(name="sum_psum", bufs=1) as sum_psum,
     ):
         offsets = held.tile([P, N // 16], U16, name="offsets")
@@ -37,11 +37,16 @@ def tile_dcn_kernel(tc, table, dense, w, offs, out):
 
         ones = held.tile([P, PIECE], F32, name="ones")
         nc.vector.memset(ones[:], 1.0)
+        w_psum = w_psum_pool.tile([P, BLOCKS + 1], F32, name="w_psum")
+        for b in range(BLOCKS + 1):
+            nc.tensor.matmul(
+                w_psum[:, b : b + 1], w_row[0:1, b * P : (b + 1) * P], ones[0:1, 0:1], start=True, stop=True
+            )
+        w_col = held.tile([P, BLOCKS + 1], F32, name="w_col")
+        nc.vector.tensor_copy(w_col[:], w_psum[:])
         w_wide = [held.tile([P, PIECE], F32, name=f"w_wide{b}") for b in range(BLOCKS + 1)]
         for b in range(BLOCKS + 1):
-            w_outer = outer_psum.tile([P, PIECE], F32, name="w_outer")
-            nc.tensor.matmul(w_outer[:], w_row[0:1, b * P : (b + 1) * P], ones[0:1, :], start=True, stop=True)
-            nc.scalar.copy(w_wide[b][:], w_outer[:])
+            nc.vector.tensor_scalar_mul(w_wide[b][:], ones[:], w_col[:, b : b + 1])
 
         def piece_of(tile, q):
             return tile[:, q * PIECE : (q + 1) * PIECE]

@@ -68,9 +68,7 @@ def tile_dcn_kernel(tc, table, dense, w, offs, out):
             nc.scalar.activation(scale[:], sums[q][:], COPY, bias=1.0)
             for b in range(BLOCKS + 1):
                 crossed = crossed_pool.tile([P, PIECE], F32, name="crossed")
-                if b < BLOCKS:
-                    nc.vector.tensor_tensor(crossed[:], looked_up(b, q), scale[:], MULT)
-                else:
-                    nc.gpsimd.tensor_tensor(crossed[:], piece_of(dense_sb, q), scale[:], MULT)
+                x0 = looked_up(b, q) if b < BLOCKS else piece_of(dense_sb, q)
+                nc.vector.tensor_tensor(crossed[:], x0, scale[:], MULT)
                 nc.scalar.activation(crossed[:], crossed[:], COPY, bias=B_CROSS)
                 nc.sync.dma_start(piece_of(out[b * P : (b + 1) * P, :], q), crossed[:])

@@ -25,6 +25,9 @@ def tile_dcn_kernel(tc, table, dense, w, offs, out):
         tc.psum_pool(name="w_psum_pool", bufs=1) as w_psum_pool,
         tc.psum_pool(name="sum_psum", bufs=1) as sum_psum,
     ):
+        def piece_of(columns, q):
+            return columns[:, q * PIECE : (q + 1) * PIECE]
+
         offsets = held.tile([P, N // 16], U16, name="offsets")
         nc.sync.dma_start(offsets[:], offs)
         windows = [held.tile([P, S], F32, name=f"window{b}") for b in range(BLOCKS)]
@@ -32,8 +35,9 @@ def tile_dcn_kernel(tc, table, dense, w, offs, out):
             nc.sync.dma_start(windows[b][:], table[b * P : (b + 1) * P, :])
         w_row = held.tile([1, C + DD], F32, name="w_row")
         nc.scalar.dma_start(w_row[:], w.rearrange("c o -> o c"))
-        dense_sb = held.tile([P, N], F32, name="dense_sb")
-        nc.scalar.dma_start(dense_sb[:], dense)
+        dense_sb = [held.tile([P, PIECE], F32, name=f"dense_sb{q}") for q in range(PIECES)]
+        for q in range(PIECES):
+            nc.sync.dma_start(dense_sb[q][:], piece_of(dense, q))
 
         ones = held.tile([P, PIECE], F32, name="ones")
         nc.vector.memset(ones[:], 1.0)
@@ -48,27 +52,24 @@ def tile_dcn_kernel(tc, table, dense, w, offs, out):
         for b in range(BLOCKS + 1):
             nc.vector.tensor_scalar_mul(w_wide[b][:], ones[:], w_col[:, b : b + 1])
 
-        def piece_of(tile, q):
-            return tile[:, q * PIECE : (q + 1) * PIECE]
-
         def looked_up(b, q):
             return windows[b][:].indirect(offsets[:, q * LIST_COLS : (q + 1) * LIST_COLS])
 
         sums = [sum_psum.tile([P, PIECE], F32, name=f"sum{q}") for q in range(PIECES)]
-        for q in range(PIECES):
-            nc.tensor.matmul(sums[q][:], w_wide[BLOCKS][:, 0:P], piece_of(dense_sb, q), start=True, stop=False)
         for b in range(BLOCKS):
             for q in range(PIECES):
                 weighted = weighted_pool.tile([P, PIECE], F32, name="weighted")
                 nc.vector.tensor_tensor(weighted[:], looked_up(b, q), w_wide[b][:], MULT)
-                nc.tensor.matmul(sums[q][:], ones[:, 0:P], weighted[:], start=False, stop=(b == BLOCKS - 1))
+                nc.tensor.matmul(sums[q][:], ones[:, 0:P], weighted[:], start=(b == 0), stop=False)
+                if b == BLOCKS - 1:
+                    nc.tensor.matmul(sums[q][:], w_wide[BLOCKS][:, 0:P], dense_sb[q][:], start=False, stop=True)
 
         for q in range(PIECES):
             scale = held.tile([P, PIECE], F32, name=f"scale{q}")
             nc.scalar.activation(scale[:], sums[q][:], COPY, bias=1.0)
             for b in range(BLOCKS + 1):
                 crossed = crossed_pool.tile([P, PIECE], F32, name="crossed")
-                x0 = looked_up(b, q) if b < BLOCKS else piece_of(dense_sb, q)
+                x0 = looked_up(b, q) if b < BLOCKS else dense_sb[q][:]
                 nc.vector.tensor_tensor(crossed[:], x0, scale[:], MULT)
                 nc.scalar.activation(crossed[:], crossed[:], COPY, bias=B_CROSS)
                 nc.sync.dma_start(piece_of(out[b * P : (b + 1) * P, :], q), crossed[:])

@@ -31,13 +31,15 @@ def tile_dcn_kernel(tc, table, dense, w, offs, out):
         offsets = held.tile([P, N // 16], U16, name="offsets")
         nc.sync.dma_start(offsets[:], offs)
         windows = [held.tile([P, S], F32, name=f"window{b}") for b in range(BLOCKS)]
-        for b in range(BLOCKS):
+        dense_sb = [held.tile([P, PIECE], F32, name=f"dense_sb{q}") for q in range(PIECES)]
+        for b in range(BLOCKS - 1):
             nc.sync.dma_start(windows[b][:], table[b * P : (b + 1) * P, :])
+        nc.sync.dma_start(dense_sb[0][:], piece_of(dense, 0))
+        nc.sync.dma_start(windows[BLOCKS - 1][:], table[(BLOCKS - 1) * P : BLOCKS * P, :])
+        for q in range(1, PIECES):
+            nc.sync.dma_start(dense_sb[q][:], piece_of(dense, q))
         w_row = held.tile([1, C + DD], F32, name="w_row")
         nc.scalar.dma_start(w_row[:], w.rearrange("c o -> o c"))
-        dense_sb = [held.tile([P, PIECE], F32, name=f"dense_sb{q}") for q in range(PIECES)]
-        for q in range(PIECES):
-            nc.sync.dma_start(dense_sb[q][:], piece_of(dense, q))
 
         ones = held.tile([P, PIECE], F32, name="ones")
         nc.vector.memset(ones[:], 1.0)
@@ -56,13 +58,19 @@ def tile_dcn_kernel(tc, table, dense, w, offs, out):
             return windows[b][:].indirect(offsets[:, q * LIST_COLS : (q + 1) * LIST_COLS])
 
         sums = [sum_psum.tile([P, PIECE], F32, name=f"sum{q}") for q in range(PIECES)]
+
+        def add_dense(q):
+            nc.tensor.matmul(sums[q][:], w_wide[BLOCKS][:, 0:P], dense_sb[q][:], start=False, stop=False)
+
         for b in range(BLOCKS):
+            if b == BLOCKS - 1:
+                add_dense(0)
             for q in range(PIECES):
                 weighted = weighted_pool.tile([P, PIECE], F32, name="weighted")
                 nc.vector.tensor_tensor(weighted[:], looked_up(b, q), w_wide[b][:], MULT)
-                nc.tensor.matmul(sums[q][:], ones[:, 0:P], weighted[:], start=(b == 0), stop=False)
-                if b == BLOCKS - 1:
-                    nc.tensor.matmul(sums[q][:], w_wide[BLOCKS][:, 0:P], dense_sb[q][:], start=False, stop=True)
+                nc.tensor.matmul(sums[q][:], ones[:, 0:P], weighted[:], start=(b == 0), stop=(b == BLOCKS - 1))
+                if b == BLOCKS - 1 and q + 1 < PIECES:
+                    add_dense(q + 1)
 
         for q in range(PIECES):
             scale = held.tile([P, PIECE], F32, name=f"scale{q}")

@@ -28,14 +28,18 @@ def tile_dcn_kernel(tc, table, dense, w, offs, out):
         def piece_of(columns, q):
             return columns[:, q * PIECE : (q + 1) * PIECE]
 
-        offsets = held.tile([P, N // 16], U16, name="offsets")
-        nc.sync.dma_start(offsets[:], offs)
         windows = [held.tile([P, S], F32, name=f"window{b}") for b in range(BLOCKS)]
+        offsets = held.tile([P, N // 16], U16, name="offsets")
         dense_sb = [held.tile([P, PIECE], F32, name=f"dense_sb{q}") for q in range(PIECES)]
-        for b in range(BLOCKS - 1):
+
+        def load_block(b):
             nc.sync.dma_start(windows[b][:], table[b * P : (b + 1) * P, :])
+
+        load_block(0)
+        nc.sync.dma_start(offsets[:], offs)
+        load_block(1)
         nc.sync.dma_start(dense_sb[0][:], piece_of(dense, 0))
-        nc.sync.dma_start(windows[BLOCKS - 1][:], table[(BLOCKS - 1) * P : BLOCKS * P, :])
+        load_block(2)
         for q in range(1, PIECES):
             nc.sync.dma_start(dense_sb[q][:], piece_of(dense, q))
         w_row = held.tile([1, C + DD], F32, name="w_row")

@@ -38,9 +38,8 @@ def tile_dcn_kernel(tc, table, dense, w, offs, out):
         load_block(0)
         nc.sync.dma_start(offsets[:], offs)
         load_block(1)
-        nc.sync.dma_start(dense_sb[0][:], piece_of(dense, 0))
         load_block(2)
-        for q in range(1, PIECES):
+        for q in range(PIECES):
             nc.sync.dma_start(dense_sb[q][:], piece_of(dense, q))
         w_row = held.tile([1, C + DD], F32, name="w_row")
         nc.scalar.dma_start(w_row[:], w.rearrange("c o -> o c"))
@@ -67,14 +66,12 @@ def tile_dcn_kernel(tc, table, dense, w, offs, out):
             nc.tensor.matmul(sums[q][:], w_wide[BLOCKS][:, 0:P], dense_sb[q][:], start=False, stop=False)
 
         for b in range(BLOCKS):
-            if b == BLOCKS - 1:
-                add_dense(0)
             for q in range(PIECES):
                 weighted = weighted_pool.tile([P, PIECE], F32, name="weighted")
                 nc.vector.tensor_tensor(weighted[:], looked_up(b, q), w_wide[b][:], MULT)
+                if b == BLOCKS - 1:
+                    add_dense(q)
                 nc.tensor.matmul(sums[q][:], ones[:, 0:P], weighted[:], start=(b == 0), stop=(b == BLOCKS - 1))
-                if b == BLOCKS - 1 and q + 1 < PIECES:
-                    add_dense(q + 1)
 
         for q in range(PIECES):
             scale = held.tile([P, PIECE], F32, name=f"scale{q}")

@@ -1,4 +1,5 @@
 import concourse.mybir as mybir
+from concourse.masks import make_identity
 
 F32 = mybir.dt.float32
 U16 = mybir.dt.uint16
@@ -11,6 +12,8 @@ B_CROSS = 0.25
 BLOCKS = C // P
 PIECE = 256
 PIECES = N // PIECE
+CHUNKS = PIECE // P
+TURNED = PIECES // 2
 LIST_COLS = PIECE // 16
 
 FLOPS = 4 * (C + DD) * N
@@ -22,7 +25,9 @@ def tile_dcn_kernel(tc, table, dense, w, offs, out):
         tc.tile_pool(name="held", bufs=1) as held,
         tc.tile_pool(name="weighted_pool", bufs=PIECES) as weighted_pool,
         tc.tile_pool(name="crossed_pool", bufs=PIECES * (BLOCKS + 1)) as crossed_pool,
-        tc.psum_pool(name="w_psum_pool", bufs=1) as w_psum_pool,
+        tc.psum_pool(name="columns_psum", bufs=1) as columns_psum,
+        tc.psum_pool(name="dense_psum", bufs=1) as dense_psum,
+        tc.psum_pool(name="back_psum", bufs=1) as back_psum,
         tc.psum_pool(name="sum_psum", bufs=1) as sum_psum,
     ):
         def piece_of(columns, q):
@@ -46,7 +51,7 @@ def tile_dcn_kernel(tc, table, dense, w, offs, out):
 
         ones = held.tile([P, PIECE], F32, name="ones")
         nc.vector.memset(ones[:], 1.0)
-        w_psum = w_psum_pool.tile([P, BLOCKS + 1], F32, name="w_psum")
+        w_psum = columns_psum.tile([P, BLOCKS + 1], F32, name="w_psum", tag="columns")
         for b in range(BLOCKS + 1):
             nc.tensor.matmul(
                 w_psum[:, b : b + 1], w_row[0:1, b * P : (b + 1) * P], ones[0:1, 0:1], start=True, stop=True
@@ -57,28 +62,87 @@ def tile_dcn_kernel(tc, table, dense, w, offs, out):
         for b in range(BLOCKS + 1):
             nc.vector.tensor_scalar_mul(w_wide[b][:], ones[:], w_col[:, b : b + 1])
 
+        identity = held.tile([P, P], F32, name="identity")
+        make_identity(nc, identity[:])
+
         def looked_up(b, q):
             return windows[b][:].indirect(offsets[:, q * LIST_COLS : (q + 1) * LIST_COLS])
 
         sums = [sum_psum.tile([P, PIECE], F32, name=f"sum{q}") for q in range(PIECES)]
-
-        def add_dense(q):
-            nc.tensor.matmul(sums[q][:], w_wide[BLOCKS][:, 0:P], dense_sb[q][:], start=False, stop=False)
-
-        for b in range(BLOCKS):
+        for b in range(BLOCKS - 1):
             for q in range(PIECES):
                 weighted = weighted_pool.tile([P, PIECE], F32, name="weighted")
                 nc.vector.tensor_tensor(weighted[:], looked_up(b, q), w_wide[b][:], MULT)
-                if b == BLOCKS - 1:
-                    add_dense(q)
-                nc.tensor.matmul(sums[q][:], ones[:, 0:P], weighted[:], start=(b == 0), stop=(b == BLOCKS - 1))
-
+                nc.tensor.matmul(sums[q][:], ones[:, 0:P], weighted[:], start=(b == 0), stop=False)
+        last_weighted = [held.tile([P, PIECE], F32, name=f"last_weighted{q}") for q in range(PIECES)]
         for q in range(PIECES):
-            scale = held.tile([P, PIECE], F32, name=f"scale{q}")
-            nc.scalar.activation(scale[:], sums[q][:], COPY, bias=1.0)
-            for b in range(BLOCKS + 1):
-                crossed = crossed_pool.tile([P, PIECE], F32, name="crossed")
-                x0 = looked_up(b, q) if b < BLOCKS else dense_sb[q][:]
-                nc.vector.tensor_tensor(crossed[:], x0, scale[:], MULT)
-                nc.scalar.activation(crossed[:], crossed[:], COPY, bias=B_CROSS)
-                nc.sync.dma_start(piece_of(out[b * P : (b + 1) * P, :], q), crossed[:])
+            nc.vector.tensor_tensor(last_weighted[q][:], looked_up(BLOCKS - 1, q), w_wide[BLOCKS - 1][:], MULT)
+
+        def close_sum(q):
+            nc.tensor.matmul(sums[q][:], w_wide[BLOCKS][:, 0:P], dense_sb[q][:], start=False, stop=False)
+            nc.tensor.matmul(sums[q][:], ones[:, 0:P], last_weighted[q][:], start=False, stop=True)
+
+        scale = [held.tile([P, PIECE], F32, name=f"scale{q}") for q in range(PIECES)]
+
+        def make_scale(q):
+            nc.scalar.activation(scale[q][:], sums[q][:], COPY, bias=1.0)
+
+        dense_t = [dense_psum.tile([P, PIECE], F32, name=f"dense_t{q}") for q in range(TURNED)]
+        columns = [columns_psum.tile([P, CHUNKS], F32, name=f"columns{q}", tag="columns") for q in range(TURNED)]
+        turned = [held.tile([P, PIECE], F32, name=f"turned{q}") for q in range(TURNED)]
+        back = [back_psum.tile([P, PIECE], F32, name=f"back{q}", tag="back") for q in range(TURNED)]
+
+        def chunk(columns_of, c):
+            return columns_of[:, c * P : (c + 1) * P]
+
+        def turn_dense(q):
+            for c in range(CHUNKS):
+                nc.tensor.transpose(chunk(dense_t[q], c), chunk(dense_sb[q], c), identity[:])
+            for c in range(CHUNKS):
+                one_row = chunk(scale[q], c)[0:1, :]
+                nc.tensor.matmul(columns[q][:, c : c + 1], one_row, ones[0:1, 0:1], start=True, stop=True)
+
+        def multiply_turned(q):
+            scale_col = held.tile([P, CHUNKS], F32, name=f"scale_col{q}")
+            nc.scalar.copy(scale_col[:], columns[q][:])
+            for c in range(CHUNKS):
+                nc.scalar.activation(chunk(turned[q], c), chunk(dense_t[q], c), COPY, scale=scale_col[:, c : c + 1])
+
+        def turn_back(q):
+            for c in range(CHUNKS):
+                nc.tensor.transpose(chunk(back[q], c), chunk(turned[q], c), identity[:])
+
+        def add_and_store(row, q, product, result):
+            nc.scalar.activation(result[:], product[:], COPY, bias=B_CROSS)
+            nc.sync.dma_start(piece_of(out[row : row + P, :], q), result[:])
+
+        def finish_turned(q):
+            crossed = crossed_pool.tile([P, PIECE], F32, name="crossed")
+            add_and_store(C, q, back[q], crossed)
+
+        def cross(b, q):
+            crossed = crossed_pool.tile([P, PIECE], F32, name="crossed")
+            x0 = looked_up(b, q) if b < BLOCKS else dense_sb[q][:]
+            nc.vector.tensor_tensor(crossed[:], x0, scale[q][:], MULT)
+            add_and_store(b * P, q, crossed, crossed)
+
+        close_sum(0)
+        make_scale(0)
+        for q in range(PIECES):
+            if q + 1 < PIECES:
+                close_sum(q + 1)
+            if 0 < q <= TURNED:
+                turn_back(q - 1)
+            if q < TURNED:
+                turn_dense(q)
+            if q + 1 < PIECES:
+                make_scale(q + 1)
+            cross(0, q)
+            if q < TURNED:
+                multiply_turned(q)
+            for b in range(1, BLOCKS):
+                cross(b, q)
+            if 0 < q <= TURNED:
+                finish_turned(q - 1)
+            if q >= TURNED:
+                cross(BLOCKS, q)

@@ -2,6 +2,7 @@ import concourse.mybir as mybir
 from concourse.masks import make_identity
 
 F32 = mybir.dt.float32
+BF16 = mybir.dt.bfloat16
 U16 = mybir.dt.uint16
 MULT = mybir.AluOpType.mult
 COPY = mybir.ActivationFunctionType.Copy
@@ -57,9 +58,9 @@ def tile_dcn_kernel(tc, table, dense, w, offs, out):
                 w_psum[:, b : b + 1], w_row[0:1, b * P : (b + 1) * P], ones[0:1, 0:1], start=True, stop=True
             )
         w_col = held.tile([P, BLOCKS + 1], F32, name="w_col")
-        nc.vector.tensor_copy(w_col[:], w_psum[:])
-        w_wide = [held.tile([P, PIECE], F32, name=f"w_wide{b}") for b in range(BLOCKS + 1)]
-        for b in range(BLOCKS + 1):
+        nc.scalar.copy(w_col[:], w_psum[:])
+        w_wide = [held.tile([P, PIECE], F32, name=f"w_wide{b}") for b in range(BLOCKS)]
+        for b in range(BLOCKS):
             nc.vector.tensor_scalar_mul(w_wide[b][:], ones[:], w_col[:, b : b + 1])
 
         identity = held.tile([P, P], F32, name="identity")
@@ -78,9 +79,16 @@ def tile_dcn_kernel(tc, table, dense, w, offs, out):
         for q in range(PIECES):
             nc.vector.tensor_tensor(last_weighted[q][:], looked_up(BLOCKS - 1, q), w_wide[BLOCKS - 1][:], MULT)
 
+        ones_bf16 = held.tile([P, P], BF16, name="ones_bf16")
+        nc.gpsimd.memset(ones_bf16[:], 1.0)
+        weighted_dense = [held.tile([P, PIECE], BF16, name=f"weighted_dense{q}") for q in range(PIECES)]
+
+        def weigh_dense(q):
+            nc.scalar.activation(weighted_dense[q][:], dense_sb[q][:], COPY, scale=w_col[:, BLOCKS : BLOCKS + 1])
+
         def close_sum(q):
-            nc.tensor.matmul(sums[q][:], w_wide[BLOCKS][:, 0:P], dense_sb[q][:], start=False, stop=False)
-            nc.tensor.matmul(sums[q][:], ones[:, 0:P], last_weighted[q][:], start=False, stop=True)
+            nc.tensor.matmul(sums[q][:], ones[:, 0:P], last_weighted[q][:], start=False, stop=False)
+            nc.tensor.matmul(sums[q][:], ones_bf16[:], weighted_dense[q][:], start=False, stop=True)
 
         scale = [held.tile([P, PIECE], F32, name=f"scale{q}") for q in range(PIECES)]
 
@@ -92,12 +100,17 @@ def tile_dcn_kernel(tc, table, dense, w, offs, out):
         turned = [held.tile([P, PIECE], F32, name=f"turned{q}") for q in range(TURNED)]
         back = [back_psum.tile([P, PIECE], F32, name=f"back{q}", tag="back") for q in range(TURNED)]
 
-        def chunk(columns_of, c):
-            return columns_of[:, c * P : (c + 1) * P]
+        def is_turned(q):
+            return 0 <= q < TURNED
+
+        def chunk(tile, c):
+            return tile[:, c * P : (c + 1) * P]
 
         def turn_dense(q):
             for c in range(CHUNKS):
                 nc.tensor.transpose(chunk(dense_t[q], c), chunk(dense_sb[q], c), identity[:])
+
+        def turn_scale(q):
             for c in range(CHUNKS):
                 one_row = chunk(scale[q], c)[0:1, :]
                 nc.tensor.matmul(columns[q][:, c : c + 1], one_row, ones[0:1, 0:1], start=True, stop=True)
@@ -126,23 +139,30 @@ def tile_dcn_kernel(tc, table, dense, w, offs, out):
             nc.vector.tensor_tensor(crossed[:], x0, scale[q][:], MULT)
             add_and_store(b * P, q, crossed, crossed)
 
-        close_sum(0)
+        def prepare(q):
+            if is_turned(q):
+                turn_dense(q)
+            weigh_dense(q)
+            close_sum(q)
+
+        prepare(0)
+        prepare(1)
         make_scale(0)
         for q in range(PIECES):
-            if q + 1 < PIECES:
-                close_sum(q + 1)
-            if 0 < q <= TURNED:
+            if is_turned(q - 1):
                 turn_back(q - 1)
-            if q < TURNED:
-                turn_dense(q)
+            if is_turned(q):
+                turn_scale(q)
+            if q + 2 < PIECES:
+                prepare(q + 2)
+            cross(0, q)
             if q + 1 < PIECES:
                 make_scale(q + 1)
-            cross(0, q)
-            if q < TURNED:
+            if is_turned(q - 1):
+                finish_turned(q - 1)
+            if is_turned(q):
                 multiply_turned(q)
             for b in range(1, BLOCKS):
                 cross(b, q)
-            if 0 < q <= TURNED:
-                finish_turned(q - 1)
-            if q >= TURNED:
+            if not is_turned(q):
                 cross(BLOCKS, q)

@@ -140,14 +140,14 @@ def tile_dcn_kernel(tc, table, dense, w, offs, out):
             add_and_store(b * P, q, crossed, crossed)
 
         def prepare(q):
-            if is_turned(q):
-                turn_dense(q)
             weigh_dense(q)
             close_sum(q)
+            if is_turned(q):
+                turn_dense(q)
 
         prepare(0)
-        prepare(1)
         make_scale(0)
+        prepare(1)
         for q in range(PIECES):
             if is_turned(q - 1):
                 turn_back(q - 1)

@@ -14,7 +14,7 @@ BLOCKS = C // P
 PIECE = 256
 PIECES = N // PIECE
 CHUNKS = PIECE // P
-TURNED = PIECES // 2
+TURNED = PIECES - 1
 LIST_COLS = PIECE // 16
 
 FLOPS = 4 * (C + DD) * N
@@ -26,8 +26,8 @@ def tile_dcn_kernel(tc, table, dense, w, offs, out):
         tc.tile_pool(name="held", bufs=1) as held,
         tc.tile_pool(name="weighted_pool", bufs=PIECES) as weighted_pool,
         tc.tile_pool(name="crossed_pool", bufs=PIECES * (BLOCKS + 1)) as crossed_pool,
-        tc.psum_pool(name="columns_psum", bufs=1) as columns_psum,
-        tc.psum_pool(name="dense_psum", bufs=1) as dense_psum,
+        tc.tile_pool(name="weighted_dense_pool", bufs=2) as weighted_dense_pool,
+        tc.psum_pool(name="turned_psum", bufs=1) as turned_psum,
         tc.psum_pool(name="back_psum", bufs=1) as back_psum,
         tc.psum_pool(name="sum_psum", bufs=1) as sum_psum,
     ):
@@ -52,13 +52,14 @@ def tile_dcn_kernel(tc, table, dense, w, offs, out):
 
         ones = held.tile([P, PIECE], F32, name="ones")
         nc.vector.memset(ones[:], 1.0)
-        w_psum = columns_psum.tile([P, BLOCKS + 1], F32, name="w_psum", tag="columns")
+        odd_bank = turned_psum.tile([P, PIECE + (BLOCKS + 1) + TURNED * CHUNKS], F32, name="odd_bank")
+        w_psum = odd_bank[:, PIECE : PIECE + BLOCKS + 1]
         for b in range(BLOCKS + 1):
             nc.tensor.matmul(
                 w_psum[:, b : b + 1], w_row[0:1, b * P : (b + 1) * P], ones[0:1, 0:1], start=True, stop=True
             )
         w_col = held.tile([P, BLOCKS + 1], F32, name="w_col")
-        nc.scalar.copy(w_col[:], w_psum[:])
+        nc.scalar.copy(w_col[:], w_psum)
         w_wide = [held.tile([P, PIECE], F32, name=f"w_wide{b}") for b in range(BLOCKS)]
         for b in range(BLOCKS):
             nc.vector.tensor_scalar_mul(w_wide[b][:], ones[:], w_col[:, b : b + 1])
@@ -81,22 +82,22 @@ def tile_dcn_kernel(tc, table, dense, w, offs, out):
 
         ones_bf16 = held.tile([P, P], BF16, name="ones_bf16")
         nc.gpsimd.memset(ones_bf16[:], 1.0)
-        weighted_dense = [held.tile([P, PIECE], BF16, name=f"weighted_dense{q}") for q in range(PIECES)]
-
-        def weigh_dense(q):
-            nc.scalar.activation(weighted_dense[q][:], dense_sb[q][:], COPY, scale=w_col[:, BLOCKS : BLOCKS + 1])
 
         def close_sum(q):
+            weighted_dense = weighted_dense_pool.tile([P, PIECE], BF16, name="weighted_dense")
+            nc.scalar.activation(weighted_dense[:], dense_sb[q][:], COPY, scale=w_col[:, BLOCKS : BLOCKS + 1])
             nc.tensor.matmul(sums[q][:], ones[:, 0:P], last_weighted[q][:], start=False, stop=False)
-            nc.tensor.matmul(sums[q][:], ones_bf16[:], weighted_dense[q][:], start=False, stop=True)
+            nc.tensor.matmul(sums[q][:], ones_bf16[:], weighted_dense[:], start=False, stop=True)
 
         scale = [held.tile([P, PIECE], F32, name=f"scale{q}") for q in range(PIECES)]
 
         def make_scale(q):
             nc.scalar.activation(scale[q][:], sums[q][:], COPY, bias=1.0)
 
-        dense_t = [dense_psum.tile([P, PIECE], F32, name=f"dense_t{q}") for q in range(TURNED)]
-        columns = [columns_psum.tile([P, CHUNKS], F32, name=f"columns{q}", tag="columns") for q in range(TURNED)]
+        even_bank = turned_psum.tile([P, PIECE], F32, name="even_bank")
+        dense_t = [(odd_bank if q % 2 else even_bank)[:, 0:PIECE] for q in range(TURNED)]
+        first_column = PIECE + BLOCKS + 1
+        columns = [odd_bank[:, first_column + q * CHUNKS : first_column + (q + 1) * CHUNKS] for q in range(TURNED)]
         turned = [held.tile([P, PIECE], F32, name=f"turned{q}") for q in range(TURNED)]
         back = [back_psum.tile([P, PIECE], F32, name=f"back{q}", tag="back") for q in range(TURNED)]
 
@@ -117,7 +118,7 @@ def tile_dcn_kernel(tc, table, dense, w, offs, out):
 
         def multiply_turned(q):
             scale_col = held.tile([P, CHUNKS], F32, name=f"scale_col{q}")
-            nc.scalar.copy(scale_col[:], columns[q][:])
+            nc.scalar.copy(scale_col[:], columns[q])
             for c in range(CHUNKS):
                 nc.scalar.activation(chunk(turned[q], c), chunk(dense_t[q], c), COPY, scale=scale_col[:, c : c + 1])
 
@@ -139,22 +140,19 @@ def tile_dcn_kernel(tc, table, dense, w, offs, out):
             nc.vector.tensor_tensor(crossed[:], x0, scale[q][:], MULT)
             add_and_store(b * P, q, crossed, crossed)
 
-        def prepare(q):
-            weigh_dense(q)
-            close_sum(q)
-            if is_turned(q):
-                turn_dense(q)
-
-        prepare(0)
+        turn_dense(0)
+        close_sum(0)
         make_scale(0)
-        prepare(1)
+        close_sum(1)
         for q in range(PIECES):
             if is_turned(q - 1):
                 turn_back(q - 1)
             if is_turned(q):
                 turn_scale(q)
+            if is_turned(q + 1):
+                turn_dense(q + 1)
             if q + 2 < PIECES:
-                prepare(q + 2)
+                close_sum(q + 2)
             cross(0, q)
             if q + 1 < PIECES:
                 make_scale(q + 1)

@@ -15,6 +15,7 @@ PIECE = 256
 PIECES = N // PIECE
 CHUNKS = PIECE // P
 TURNED = PIECES - 1
+BANK = PIECE + (BLOCKS + 1) + CHUNKS
 LIST_COLS = PIECE // 16
 
 FLOPS = 4 * (C + DD) * N
@@ -52,7 +53,7 @@ def tile_dcn_kernel(tc, table, dense, w, offs, out):
 
         ones = held.tile([P, PIECE], F32, name="ones")
         nc.vector.memset(ones[:], 1.0)
-        odd_bank = turned_psum.tile([P, PIECE + (BLOCKS + 1) + TURNED * CHUNKS], F32, name="odd_bank")
+        odd_bank = turned_psum.tile([P, BANK], F32, name="odd_bank")
         w_psum = odd_bank[:, PIECE : PIECE + BLOCKS + 1]
         for b in range(BLOCKS + 1):
             nc.tensor.matmul(
@@ -83,6 +84,13 @@ def tile_dcn_kernel(tc, table, dense, w, offs, out):
         ones_bf16 = held.tile([P, P], BF16, name="ones_bf16")
         nc.gpsimd.memset(ones_bf16[:], 1.0)
 
+        w_dense_wide = held.tile([P, P], F32, name="w_dense_wide")
+        nc.vector.tensor_scalar_mul(w_dense_wide[:], ones[:, 0:P], w_col[:, BLOCKS : BLOCKS + 1])
+
+        def close_first_sum():
+            nc.tensor.matmul(sums[0][:], w_dense_wide[:], dense_sb[0][:], start=False, stop=False)
+            nc.tensor.matmul(sums[0][:], ones[:, 0:P], last_weighted[0][:], start=False, stop=True)
+
         def close_sum(q):
             weighted_dense = weighted_dense_pool.tile([P, PIECE], BF16, name="weighted_dense")
             nc.scalar.activation(weighted_dense[:], dense_sb[q][:], COPY, scale=w_col[:, BLOCKS : BLOCKS + 1])
@@ -94,10 +102,10 @@ def tile_dcn_kernel(tc, table, dense, w, offs, out):
         def make_scale(q):
             nc.scalar.activation(scale[q][:], sums[q][:], COPY, bias=1.0)
 
-        even_bank = turned_psum.tile([P, PIECE], F32, name="even_bank")
-        dense_t = [(odd_bank if q % 2 else even_bank)[:, 0:PIECE] for q in range(TURNED)]
-        first_column = PIECE + BLOCKS + 1
-        columns = [odd_bank[:, first_column + q * CHUNKS : first_column + (q + 1) * CHUNKS] for q in range(TURNED)]
+        even_bank = turned_psum.tile([P, BANK], F32, name="even_bank")
+        bank = [odd_bank if q % 2 else even_bank for q in range(TURNED)]
+        dense_t = [bank[q][:, 0:PIECE] for q in range(TURNED)]
+        columns = [bank[q][:, BANK - CHUNKS : BANK] for q in range(TURNED)]
         turned = [held.tile([P, PIECE], F32, name=f"turned{q}") for q in range(TURNED)]
         back = [back_psum.tile([P, PIECE], F32, name=f"back{q}", tag="back") for q in range(TURNED)]
 
@@ -140,8 +148,7 @@ def tile_dcn_kernel(tc, table, dense, w, offs, out):
             nc.vector.tensor_tensor(crossed[:], x0, scale[q][:], MULT)
             add_and_store(b * P, q, crossed, crossed)
 
-        turn_dense(0)
-        close_sum(0)
+        close_first_sum()
         make_scale(0)
         close_sum(1)
         for q in range(PIECES):
@@ -149,8 +156,7 @@ def tile_dcn_kernel(tc, table, dense, w, offs, out):
                 turn_back(q - 1)
             if is_turned(q):
                 turn_scale(q)
-            if is_turned(q + 1):
-                turn_dense(q + 1)
+                turn_dense(q)
             if q + 2 < PIECES:
                 close_sum(q + 2)
             cross(0, q)

import concourse.mybir as mybir
from concourse.masks import make_identity

F32 = mybir.dt.float32
BF16 = mybir.dt.bfloat16
U16 = mybir.dt.uint16
MULT = mybir.AluOpType.mult
COPY = mybir.ActivationFunctionType.Copy

P = 128
C, DD, S, N = 384, 128, 4096, 1024
B_CROSS = 0.25
BLOCKS = C // P
PIECE = 256
PIECES = N // PIECE
CHUNKS = PIECE // P
TURNED = PIECES - 1
BANK = PIECE + (BLOCKS + 1) + CHUNKS
LIST_COLS = PIECE // 16

FLOPS = 4 * (C + DD) * N


def tile_dcn_kernel(tc, table, dense, w, offs, out):
    nc = tc.nc
    with (
        tc.tile_pool(name="held", bufs=1) as held,
        tc.tile_pool(name="weighted_pool", bufs=PIECES) as weighted_pool,
        tc.tile_pool(name="crossed_pool", bufs=PIECES * (BLOCKS + 1)) as crossed_pool,
        tc.tile_pool(name="weighted_dense_pool", bufs=2) as weighted_dense_pool,
        tc.psum_pool(name="turned_psum", bufs=1) as turned_psum,
        tc.psum_pool(name="back_psum", bufs=1) as back_psum,
        tc.psum_pool(name="sum_psum", bufs=1) as sum_psum,
    ):
        def piece_of(columns, q):
            return columns[:, q * PIECE : (q + 1) * PIECE]

        windows = [held.tile([P, S], F32, name=f"window{b}") for b in range(BLOCKS)]
        offsets = held.tile([P, N // 16], U16, name="offsets")
        dense_sb = [held.tile([P, PIECE], F32, name=f"dense_sb{q}") for q in range(PIECES)]

        def load_block(b):
            nc.sync.dma_start(windows[b][:], table[b * P : (b + 1) * P, :])

        load_block(0)
        nc.sync.dma_start(offsets[:], offs)
        load_block(1)
        load_block(2)
        for q in range(PIECES):
            nc.sync.dma_start(dense_sb[q][:], piece_of(dense, q))
        w_row = held.tile([1, C + DD], F32, name="w_row")
        nc.scalar.dma_start(w_row[:], w.rearrange("c o -> o c"))

        ones = held.tile([P, PIECE], F32, name="ones")
        nc.vector.memset(ones[:], 1.0)
        odd_bank = turned_psum.tile([P, BANK], F32, name="odd_bank")
        w_psum = odd_bank[:, PIECE : PIECE + BLOCKS + 1]
        for b in range(BLOCKS + 1):
            nc.tensor.matmul(
                w_psum[:, b : b + 1], w_row[0:1, b * P : (b + 1) * P], ones[0:1, 0:1], start=True, stop=True
            )
        w_col = held.tile([P, BLOCKS + 1], F32, name="w_col")
        nc.scalar.copy(w_col[:], w_psum)
        w_wide = [held.tile([P, PIECE], F32, name=f"w_wide{b}") for b in range(BLOCKS)]
        for b in range(BLOCKS):
            nc.vector.tensor_scalar_mul(w_wide[b][:], ones[:], w_col[:, b : b + 1])

        identity = held.tile([P, P], F32, name="identity")
        make_identity(nc, identity[:])

        def looked_up(b, q):
            return windows[b][:].indirect(offsets[:, q * LIST_COLS : (q + 1) * LIST_COLS])

        sums = [sum_psum.tile([P, PIECE], F32, name=f"sum{q}") for q in range(PIECES)]
        for b in range(BLOCKS - 1):
            for q in range(PIECES):
                weighted = weighted_pool.tile([P, PIECE], F32, name="weighted")
                nc.vector.tensor_tensor(weighted[:], looked_up(b, q), w_wide[b][:], MULT)
                nc.tensor.matmul(sums[q][:], ones[:, 0:P], weighted[:], start=(b == 0), stop=False)
        last_weighted = [held.tile([P, PIECE], F32, name=f"last_weighted{q}") for q in range(PIECES)]
        for q in range(PIECES):
            nc.vector.tensor_tensor(last_weighted[q][:], looked_up(BLOCKS - 1, q), w_wide[BLOCKS - 1][:], MULT)

        ones_bf16 = held.tile([P, P], BF16, name="ones_bf16")
        nc.gpsimd.memset(ones_bf16[:], 1.0)

        w_dense_wide = held.tile([P, P], F32, name="w_dense_wide")
        nc.vector.tensor_scalar_mul(w_dense_wide[:], ones[:, 0:P], w_col[:, BLOCKS : BLOCKS + 1])

        def close_first_sum():
            nc.tensor.matmul(sums[0][:], w_dense_wide[:], dense_sb[0][:], start=False, stop=False)
            nc.tensor.matmul(sums[0][:], ones[:, 0:P], last_weighted[0][:], start=False, stop=True)

        def close_sum(q):
            weighted_dense = weighted_dense_pool.tile([P, PIECE], BF16, name="weighted_dense")
            nc.scalar.activation(weighted_dense[:], dense_sb[q][:], COPY, scale=w_col[:, BLOCKS : BLOCKS + 1])
            nc.tensor.matmul(sums[q][:], ones[:, 0:P], last_weighted[q][:], start=False, stop=False)
            nc.tensor.matmul(sums[q][:], ones_bf16[:], weighted_dense[:], start=False, stop=True)

        scale = [held.tile([P, PIECE], F32, name=f"scale{q}") for q in range(PIECES)]

        def make_scale(q):
            nc.scalar.activation(scale[q][:], sums[q][:], COPY, bias=1.0)

        even_bank = turned_psum.tile([P, BANK], F32, name="even_bank")
        bank = [odd_bank if q % 2 else even_bank for q in range(TURNED)]
        dense_t = [bank[q][:, 0:PIECE] for q in range(TURNED)]
        columns = [bank[q][:, BANK - CHUNKS : BANK] for q in range(TURNED)]
        turned = [held.tile([P, PIECE], F32, name=f"turned{q}") for q in range(TURNED)]
        back = [back_psum.tile([P, PIECE], F32, name=f"back{q}", tag="back") for q in range(TURNED)]

        def is_turned(q):
            return 0 <= q < TURNED

        def chunk(tile, c):
            return tile[:, c * P : (c + 1) * P]

        def turn_dense(q):
            for c in range(CHUNKS):
                nc.tensor.transpose(chunk(dense_t[q], c), chunk(dense_sb[q], c), identity[:])

        def turn_scale(q):
            for c in range(CHUNKS):
                one_row = chunk(scale[q], c)[0:1, :]
                nc.tensor.matmul(columns[q][:, c : c + 1], one_row, ones[0:1, 0:1], start=True, stop=True)

        def multiply_turned(q):
            scale_col = held.tile([P, CHUNKS], F32, name=f"scale_col{q}")
            nc.scalar.copy(scale_col[:], columns[q])
            for c in range(CHUNKS):
                nc.scalar.activation(chunk(turned[q], c), chunk(dense_t[q], c), COPY, scale=scale_col[:, c : c + 1])

        def turn_back(q):
            for c in range(CHUNKS):
                nc.tensor.transpose(chunk(back[q], c), chunk(turned[q], c), identity[:])

        def add_and_store(row, q, product, result):
            nc.scalar.activation(result[:], product[:], COPY, bias=B_CROSS)
            nc.sync.dma_start(piece_of(out[row : row + P, :], q), result[:])

        def finish_turned(q):
            crossed = crossed_pool.tile([P, PIECE], F32, name="crossed")
            add_and_store(C, q, back[q], crossed)

        def cross(b, q):
            crossed = crossed_pool.tile([P, PIECE], F32, name="crossed")
            x0 = looked_up(b, q) if b < BLOCKS else dense_sb[q][:]
            nc.vector.tensor_tensor(crossed[:], x0, scale[q][:], MULT)
            add_and_store(b * P, q, crossed, crossed)

        close_first_sum()
        make_scale(0)
        close_sum(1)
        for q in range(PIECES):
            if is_turned(q - 1):
                turn_back(q - 1)
            if is_turned(q):
                turn_scale(q)
                turn_dense(q)
            if q + 2 < PIECES:
                close_sum(q + 2)
            cross(0, q)
            if q + 1 < PIECES:
                make_scale(q + 1)
            if is_turned(q - 1):
                finish_turned(q - 1)
            if is_turned(q):
                multiply_turned(q)
            for b in range(1, BLOCKS):
                cross(b, q)
            if not is_turned(q):
                cross(BLOCKS, q)
